import numpy as np
import ml_dtypes


def mxq(x, axis, fmt="e4m3"):
    dtype, down = {"e4m3": (ml_dtypes.float8_e4m3fn, 7), "e5m2": (ml_dtypes.float8_e5m2, 14)}[fmt]
    v = np.moveaxis(np.asarray(x, np.float32).astype(ml_dtypes.bfloat16).astype(np.float64), axis, -1)
    blocks = v.reshape(v.shape[:-1] + (-1, 32))
    amax = np.abs(blocks).max(-1, keepdims=True)
    byte = np.maximum(np.where(amax > 0, np.frexp(amax)[1] - 1 + 127, 0) - down, 1)
    scale = np.exp2(byte - 127.0)
    codes = (blocks / scale).astype(np.float32).astype(dtype).astype(np.float64)
    return np.moveaxis((codes * scale).reshape(v.shape), -1, axis)


WIDE = False


def mx_kscale(k):
    if not WIDE:
        return np.ones(k)
    levels = np.array([10, -10, 5, -5, 0])
    a = np.random.permutation(np.resize(levels, k // 512 * 4)).reshape(k // 512, 4)
    idx = np.arange(k)
    return np.exp2(a[idx // 512, idx % 128 // 32])


BF16 = ml_dtypes.bfloat16


def bf(x):
    return np.asarray(x, np.float32).astype(BF16)


def f64(x):
    return np.asarray(x).astype(np.float64)


E2M1 = np.array([0.0, 0.5, 1.0, 1.5, 2.0, 3.0, 4.0, 6.0, -0.0, -0.5, -1.0, -1.5, -2.0, -3.0, -4.0, -6.0])


def pack_weight(w, fmt):
    k, n = w.shape
    w = f64(bf(w)).reshape(k // 32, 32, n)
    amax = np.abs(w).max(1)
    if fmt == "e4m3":
        byte = np.frexp(amax)[1] - 1 + 127 - 7
    else:
        mant, ex = np.frexp(amax / 6.0)
        byte = np.where(mant > 0.5, ex, ex - 1) + 127
    byte = np.clip(np.where(amax > 0, byte, 1), 1, 254)
    scaled = (w * np.exp2(127.0 - byte)[:, None, :]).reshape(k, n).astype(np.float32)
    by_word = np.ascontiguousarray(scaled.reshape(k // 512, 128, 4, n).transpose(0, 1, 3, 2))
    if fmt == "e4m3":
        words = by_word.astype(ml_dtypes.float8_e4m3fn).view(np.uint8)
    else:
        c = by_word.astype(ml_dtypes.float4_e2m1fn).view(np.uint8) & 0xF
        words = c[..., 0::2] | (c[..., 1::2] << 4)
    return np.ascontiguousarray(words), np.ascontiguousarray(byte.astype(np.uint8).reshape(k // 512, 16, n))


def unpack_weight(words, scales, fmt):
    g, p, n, _ = words.shape
    if fmt == "e4m3":
        vals = np.ascontiguousarray(words).view(ml_dtypes.float8_e4m3fn).astype(np.float64)
    else:
        nib = np.empty((g, p, n, 4), np.uint8)
        nib[..., 0::2] = words & 0xF
        nib[..., 1::2] = words >> 4
        vals = E2M1[nib]
    vals = vals * np.repeat(np.exp2(scales.astype(np.float64) - 127.0), 8, axis=1)[..., None]
    return vals.transpose(0, 1, 3, 2).reshape(g * 512, n)


B, H, Wd, C_IN, KH, KW, OUT = 2, 8, 8, 456, 3, 3, 4097
HCAT = (C_IN - 1) * KH * KW + 1
CURV = 1.0
FMT = "e4m3"


def chan_scale():
    lv = np.unique(mx_kscale(HCAT))
    cyc = np.roll(np.concatenate([lv, lv[::-1]]), -(len(lv) // 2))
    return cyc[(np.arange(C_IN - 1) * len(cyc)) // (C_IN - 1)]


def setup_inputs():
    u = chan_scale()
    v = np.random.standard_normal((B, H, Wd, C_IN - 1)) * 0.5
    t = np.sqrt(1.0 / CURV + np.sum(v * v, axis=-1, keepdims=True))
    s = np.concatenate([np.ones(1), np.tile(u, KH * KW)])
    w = np.random.standard_normal((OUT - 1, HCAT)) * (0.7 / np.sqrt(HCAT)) / s
    words, scales = pack_weight(np.ascontiguousarray(w.T), FMT)
    return {"x": bf(np.concatenate([t, v * u], axis=-1)),
            "W_words": words,
            "W_scales": scales,
            "b": bf(np.random.standard_normal(OUT - 1) * 0.1)}


def reference(x, W_words, W_scales, b):
    c = CURV
    x = f64(x)
    Bn, Hn, Wn, C = x.shape
    xp = np.pad(x, ((0, 0), (1, 1), (1, 1), (0, 0)), mode="edge")
    slabs = [xp[:, i:i + Hn, j:j + Wn, :] for i in range(KH) for j in range(KW)]
    patches = np.stack(slabs, axis=3)
    N = KH * KW
    t_cat = np.sqrt(np.sum(patches[..., 0] ** 2, axis=-1) - (N - 1) / c)
    sp = patches[..., 1:].reshape(Bn, Hn, Wn, N * (C - 1))
    h = np.concatenate([t_cat[..., None], sp], axis=-1)
    z = (mxq(h, 3, "e4m3") @ unpack_weight(W_words, W_scales, FMT)) + f64(b)
    t_out = np.sqrt(1.0 / c + np.sum(z * z, axis=-1, keepdims=True))
    return np.concatenate([t_out, z], axis=-1)

@@ -1,0 +1,180 @@
+from contextlib import ExitStack
+
+import concourse.mybir as mybir
+from concourse.masks import make_identity
+
+F32 = mybir.dt.float32
+BF16 = mybir.dt.bfloat16
+U8 = mybir.dt.uint8
+U32 = mybir.dt.uint32
+I32 = mybir.dt.int32
+FP8X4 = mybir.dt.float8_e4m3fn_x4
+ACT = mybir.ActivationFunctionType
+ALU = mybir.AluOpType
+AX = mybir.AxisListType
+
+P = 128
+C_IN = 456
+SPACE = 455
+GROUPS = 8
+BANK = 512
+N_OUT = 4096
+XBASE = 456
+XCOLS = 342
+ZCOL = 8
+
+FLOPS = 2 * 128 * 4096 * 4096
+
+
+def tile_hypconvhyperboloid_w_kernel(tc, x, W_words, W_scales, b, out):
+    nc = tc.nc
+    x_rows = x.flatten_outer_dims()
+    out_rows = out.flatten_outer_dims()
+    with ExitStack() as ctx:
+        keep = ctx.enter_context(tc.tile_pool(name="keep", bufs=1))
+        psum = ctx.enter_context(tc.psum_pool(name="psum", bufs=8))
+        ctx.enter_context(tc.manual_schedule())
+
+        planes = keep.tile([P, 2, N_OUT], U8, align_bytes=64)
+        w = [keep.tile([P, N_OUT], U32, name="w%d" % g, align_bytes=64) for g in range(GROUPS)]
+        x_sb = keep.tile([P, C_IN], BF16)
+        b8 = keep.tile([P, BANK], BF16)
+        consts = keep.tile([P, 2], F32)
+        warm = keep.tile([P, 1], F32)
+        ident = keep.tile([P, P], BF16)
+        ipad = keep.tile([P, 2, 10, 10], BF16)
+        taps = keep.tile([P, 9, P], BF16)
+        counts = keep.tile([P, P], F32)
+        xs = keep.tile([P, 4, XCOLS], BF16)
+        tsq = keep.tile([P, 1], F32)
+        grouped = keep.tile([P, GROUPS, P, 4], BF16, align_bytes=64)
+        hq = keep.tile([P, GROUPS * P], U32, align_bytes=64)
+        hs = keep.tile([P, GROUPS * P], U8, align_bytes=64)
+        out_sb = keep.tile([P, ZCOL + N_OUT], F32)
+        junk = keep.tile([P, BANK], F32)
+        ssq = keep.tile([P, GROUPS], F32)
+        pre0 = keep.tile([P, 1], F32)
+        pre = keep.tile([P, 1], F32)
+
+        nc.vector.memset(planes[:, 0, :].bitcast(I32), 0)
+        nc.vector.memset(planes[:, 1, :].bitcast(I32), 0)
+        nc.scalar.dma_start(out=x_sb[:], in_=x_rows)
+        make_identity(nc, ident[:])
+        nc.gpsimd.memset(b8[:].bitcast(F32), 0.0)
+        nc.gpsimd.memset(consts[:, 0:1], -8.0)
+        nc.gpsimd.memset(consts[:, 1:2], 1.0)
+        nc.scalar.dma_start(out=b8[0:8, :], in_=b.rearrange("(j n) -> j n", j=8))
+        nc.scalar.activation(out=warm[:], in_=consts[:, 1:2], func=ACT.Sqrt)
+        for half in range(2):
+            for quad in (0, 2, 1, 3):
+                nc.sync.dma_start(
+                    out=planes[32 * quad : 32 * quad + 16, half, :].bitcast(I32),
+                    in_=W_scales[4 * half : 4 * half + 4, 4 * quad : 4 * quad + 4, :].bitcast(I32),
+                )
+        for g in range(GROUPS - 1):
+            nc.sync.dma_start(
+                out=w[g][:].bitcast(I32),
+                in_=W_words[g].rearrange("p n t -> p (n t)").bitcast(I32),
+            )
+        for j in range(7, -1, -1):
+            nc.sync.dma_start(
+                out=w[7][:, BANK * j : BANK * (j + 1)].bitcast(I32),
+                in_=W_words[7, :, BANK * j : BANK * (j + 1), :].rearrange("p n t -> p (n t)").bitcast(I32),
+            )
+
+        nc.vector.memset(xs[:].rearrange("p f c -> p (f c)").bitcast(I32), 0)
+        ident4 = ident[:].rearrange("p (b r q) -> p b r q", b=2, r=8)
+        nc.vector.tensor_copy(out=ipad[:, :, 1:9, 1:9], in_=ident4)
+        nc.vector.tensor_copy(out=ipad[:, :, 1:9, 0:1], in_=ident4[:, :, :, 0:1])
+        nc.vector.tensor_copy(out=ipad[:, :, 1:9, 9:10], in_=ident4[:, :, :, 7:8])
+        nc.vector.tensor_copy(out=ipad[:, :, 0:1, :], in_=ipad[:, :, 1:2, :])
+        nc.vector.tensor_copy(out=ipad[:, :, 9:10, :], in_=ipad[:, :, 8:9, :])
+        for n in range(9):
+            nc.vector.tensor_copy(
+                out=taps[:, n, :].rearrange("p (b r q) -> p b r q", b=2, r=8),
+                in_=ipad[:, :, n // 3 : n // 3 + 8, n % 3 : n % 3 + 8],
+            )
+
+        nc.vector.tensor_copy(
+            out=xs[:, :, XBASE // 4 : XBASE // 4 + C_IN // 4],
+            in_=x_sb[:].rearrange("p (c f) -> p f c", f=4),
+        )
+        nc.vector.memset(xs[:, 0, XBASE // 4 : XBASE // 4 + 1], 0.0)
+        nc.vector.tensor_tensor(out=tsq[:], in0=x_sb[:, 0:1], in1=x_sb[:, 0:1], op=ALU.mult)
+        nc.vector.tensor_reduce(out=counts[:], in_=taps[:].rearrange("p n x -> p x n"), axis=AX.X, op=ALU.add)
+
+        def gather_group(g):
+            hp = psum.tile([P, 4, P], F32, tag="bank", name="hp%d" % g)
+            for t in range(4):
+                for n in (g, g + 1):
+                    s = XBASE + 512 * g + t - SPACE * n
+                    nc.tensor.matmul(
+                        out=hp[:, t, :],
+                        lhsT=xs[:, s % 4, s // 4 : s // 4 + P],
+                        rhs=taps[:, n, :],
+                        start=(n == g),
+                        stop=(n == g + 1),
+                    )
+            src = hp[:].rearrange("p t x -> p x t")
+            if g % 2 == 0:
+                nc.vector.tensor_copy(out=grouped[:, g], in_=src)
+            else:
+                nc.scalar.copy(out=grouped[:, g], in_=src)
+
+        gather_group(0)
+        gather_group(1)
+        tp = psum.tile([P, BANK], F32, tag="bank")
+        nc.tensor.matmul(
+            out=tp[:, 0:P], lhsT=tsq[:, 0:1].to_broadcast([P, P]), rhs=counts[:], start=True, stop=True
+        )
+        nc.scalar.activation(
+            out=grouped[0:1, 0, :, 0], in_=tp[0:1, 0:P], func=ACT.Sqrt, bias=consts[0:1, 0:1], scale=1.0
+        )
+        for g in range(2, GROUPS):
+            gather_group(g)
+        for half in range(2):
+            nc.vector.quantize_mx(
+                out=hq[:, 512 * half : 512 * (half + 1)].bitcast(FP8X4),
+                scales=hs[:, 512 * half : 512 * (half + 1)],
+                in_=grouped[:, 4 * half : 4 * half + 4].rearrange("p g x t -> p (g x t)"),
+            )
+
+        for j in range(8):
+            bp = psum.tile([P, BANK], F32, tag="bank", name="bp%d" % j)
+            nc.tensor.matmul(
+                out=bp[:], lhsT=ident[:, j : j + 1].to_broadcast([P, P]), rhs=b8[:], start=True, stop=True
+            )
+            dst = out_sb[:, ZCOL + BANK * j : ZCOL + BANK * (j + 1)]
+            if j % 2 == 0:
+                nc.vector.tensor_copy(out=dst, in_=bp[:])
+            else:
+                nc.scalar.copy(out=dst, in_=bp[:])
+
+        acc = [psum.tile([P, BANK], F32, tag="bank", name="acc%d" % j) for j in range(8)]
+        for g in range(GROUPS):
+            for j in range(7, -1, -1):
+                nc.tensor.matmul_mx(
+                    out=acc[j][:],
+                    lhsT=hq[:, P * g : P * (g + 1)].bitcast(FP8X4),
+                    lhsT_scale=hs[:, P * g : P * (g + 1)],
+                    rhs=w[g][:, BANK * j : BANK * (j + 1)].bitcast(FP8X4),
+                    rhs_scale=planes[4 * (g % 4) : P, g // 4, BANK * j : BANK * (j + 1)],
+                    start=(g == 0),
+                    stop=(g == GROUPS - 1),
+                )
+
+        for i, j in enumerate(range(7, -1, -1)):
+            z = out_sb[:, ZCOL + BANK * j : ZCOL + BANK * (j + 1)]
+            nc.vector.tensor_tensor(out=z, in0=acc[j][:], in1=z, op=ALU.add)
+            nc.scalar.activation(out=junk[:], in_=z, func=ACT.Square, accum_out=ssq[:, i : i + 1])
+            if j in (6, 4, 2):
+                nc.sync.dma_start(
+                    out=out_rows[:, 1 + BANK * j : 1 + BANK * (j + 2)],
+                    in_=out_sb[:, ZCOL + BANK * j : ZCOL + BANK * (j + 2)],
+                )
+        nc.vector.tensor_reduce(out=pre0[:], in_=ssq[:, 0:7], axis=AX.X, op=ALU.add)
+        nc.vector.tensor_scalar_add(out=pre[:], in0=pre0[:], scalar1=1.0)
+        nc.scalar.activation(
+            out=out_sb[:, ZCOL - 1 : ZCOL], in_=ssq[:, 7:8], func=ACT.Sqrt, bias=pre[:, 0:1], scale=1.0
+        )
+        nc.sync.dma_start(out=out_rows[:, 0 : 1 + 2 * BANK], in_=out_sb[:, ZCOL - 1 : ZCOL + 2 * BANK])

@@ -67,9 +67,9 @@ def tile_hypconvhyperboloid_w_kernel(tc, x, W_words, W_scales, b, out):
         nc.scalar.activation(out=warm[:], in_=consts[:, 1:2], func=ACT.Sqrt)
         for half in range(2):
             for quad in (0, 2, 1, 3):
-                nc.sync.dma_start(
-                    out=planes[32 * quad : 32 * quad + 16, half, :].bitcast(I32),
-                    in_=W_scales[4 * half : 4 * half + 4, 4 * quad : 4 * quad + 4, :].bitcast(I32),
+                nc.gpsimd.dma_start(
+                    out=planes[32 * quad : 32 * quad + 16, half, :].bitcast(F32),
+                    in_=W_scales[4 * half : 4 * half + 4, 4 * quad : 4 * quad + 4, :].bitcast(F32),
                 )
         for g in range(GROUPS - 1):
             nc.sync.dma_start(

@@ -22,6 +22,8 @@ N_OUT = 4096
 XBASE = 456
 XCOLS = 342
 ZCOL = 8
+WHOLE = 6
+CHUNKS = ((3072, 4096), (2048, 3072), (1024, 2048), (512, 1024), (0, 512))
 
 FLOPS = 2 * 128 * 4096 * 4096
 
@@ -51,7 +53,7 @@ def tile_hypconvhyperboloid_w_kernel(tc, x, W_words, W_scales, b, out):
         hq = keep.tile([P, GROUPS * P], U32, align_bytes=64)
         hs = keep.tile([P, GROUPS * P], U8, align_bytes=64)
         out_sb = keep.tile([P, ZCOL + N_OUT], F32)
-        junk = keep.tile([P, BANK], F32)
+        junk = keep.tile([P, 2 * BANK], F32)
         ssq = keep.tile([P, GROUPS], F32)
         pre0 = keep.tile([P, 1], F32)
         pre = keep.tile([P, 1], F32)
@@ -65,22 +67,24 @@ def tile_hypconvhyperboloid_w_kernel(tc, x, W_words, W_scales, b, out):
         nc.gpsimd.memset(consts[:, 1:2], 1.0)
         nc.scalar.dma_start(out=b8[0:8, :], in_=b.rearrange("(j n) -> j n", j=8))
         nc.scalar.activation(out=warm[:], in_=consts[:, 1:2], func=ACT.Sqrt)
+        def load_words(g, lo, hi):
+            nc.sync.dma_start(
+                out=w[g][:, lo:hi].bitcast(I32),
+                in_=W_words[g, :, lo:hi, :].rearrange("p n t -> p (n t)").bitcast(I32),
+            )
+
+        load_words(0, 0, N_OUT)
         for half in range(2):
             for quad in (0, 2, 1, 3):
-                nc.gpsimd.dma_start(
-                    out=planes[32 * quad : 32 * quad + 16, half, :].bitcast(F32),
-                    in_=W_scales[4 * half : 4 * half + 4, 4 * quad : 4 * quad + 4, :].bitcast(F32),
+                nc.sync.dma_start(
+                    out=planes[32 * quad : 32 * quad + 16, half, :].bitcast(I32),
+                    in_=W_scales[4 * half : 4 * half + 4, 4 * quad : 4 * quad + 4, :].bitcast(I32),
                 )
-        for g in range(GROUPS - 1):
-            nc.sync.dma_start(
-                out=w[g][:].bitcast(I32),
-                in_=W_words[g].rearrange("p n t -> p (n t)").bitcast(I32),
-            )
-        for j in range(7, -1, -1):
-            nc.sync.dma_start(
-                out=w[7][:, BANK * j : BANK * (j + 1)].bitcast(I32),
-                in_=W_words[7, :, BANK * j : BANK * (j + 1), :].rearrange("p n t -> p (n t)").bitcast(I32),
-            )
+        for g in range(1, WHOLE):
+            load_words(g, 0, N_OUT)
+        for lo, hi in CHUNKS:
+            for g in range(WHOLE, GROUPS):
+                load_words(g, lo, hi)
 
         nc.vector.memset(xs[:].rearrange("p f c -> p (f c)").bitcast(I32), 0)
         ident4 = ident[:].rearrange("p (b r q) -> p b r q", b=2, r=8)
@@ -151,30 +155,42 @@ def tile_hypconvhyperboloid_w_kernel(tc, x, W_words, W_scales, b, out):
                 nc.scalar.copy(out=dst, in_=bp[:])
 
         acc = [psum.tile([P, BANK], F32, tag="bank", name="acc%d" % j) for j in range(8)]
-        for g in range(GROUPS):
-            for j in range(7, -1, -1):
-                nc.tensor.matmul_mx(
-                    out=acc[j][:],
-                    lhsT=hq[:, P * g : P * (g + 1)].bitcast(FP8X4),
-                    lhsT_scale=hs[:, P * g : P * (g + 1)],
-                    rhs=w[g][:, BANK * j : BANK * (j + 1)].bitcast(FP8X4),
-                    rhs_scale=planes[4 * (g % 4) : P, g // 4, BANK * j : BANK * (j + 1)],
-                    start=(g == 0),
-                    stop=(g == GROUPS - 1),
-                )
 
-        for i, j in enumerate(range(7, -1, -1)):
-            z = out_sb[:, ZCOL + BANK * j : ZCOL + BANK * (j + 1)]
-            nc.vector.tensor_tensor(out=z, in0=acc[j][:], in1=z, op=ALU.add)
-            nc.scalar.activation(out=junk[:], in_=z, func=ACT.Square, accum_out=ssq[:, i : i + 1])
-            if j in (6, 4, 2):
-                nc.sync.dma_start(
-                    out=out_rows[:, 1 + BANK * j : 1 + BANK * (j + 2)],
-                    in_=out_sb[:, ZCOL + BANK * j : ZCOL + BANK * (j + 2)],
-                )
-        nc.vector.tensor_reduce(out=pre0[:], in_=ssq[:, 0:7], axis=AX.X, op=ALU.add)
+        def mx_pass(g, j):
+            nc.tensor.matmul_mx(
+                out=acc[j][:],
+                lhsT=hq[:, P * g : P * (g + 1)].bitcast(FP8X4),
+                lhsT_scale=hs[:, P * g : P * (g + 1)],
+                rhs=w[g][:, BANK * j : BANK * (j + 1)].bitcast(FP8X4),
+                rhs_scale=planes[4 * (g % 4) : P, g // 4, BANK * j : BANK * (j + 1)],
+                start=(g == 0),
+                stop=(g == GROUPS - 1),
+            )
+
+        for g in range(WHOLE):
+            for j in range(7, -1, -1):
+                mx_pass(g, j)
+
+        last = len(CHUNKS) - 1
+        for i, (lo, hi) in enumerate(CHUNKS):
+            banks = range(hi // BANK - 1, lo // BANK - 1, -1)
+            for g in range(WHOLE, GROUPS):
+                for j in banks:
+                    mx_pass(g, j)
+            for j in banks:
+                z = out_sb[:, ZCOL + BANK * j : ZCOL + BANK * (j + 1)]
+                nc.vector.tensor_tensor(out=z, in0=acc[j][:], in1=z, op=ALU.add)
+            nc.scalar.activation(
+                out=junk[:, 0 : hi - lo],
+                in_=out_sb[:, ZCOL + lo : ZCOL + hi],
+                func=ACT.Square,
+                accum_out=ssq[:, i : i + 1],
+            )
+            if i < last - 1:
+                nc.sync.dma_start(out=out_rows[:, 1 + lo : 1 + hi], in_=out_sb[:, ZCOL + lo : ZCOL + hi])
+        nc.vector.tensor_reduce(out=pre0[:], in_=ssq[:, 0:last], axis=AX.X, op=ALU.add)
         nc.vector.tensor_scalar_add(out=pre[:], in0=pre0[:], scalar1=1.0)
         nc.scalar.activation(
-            out=out_sb[:, ZCOL - 1 : ZCOL], in_=ssq[:, 7:8], func=ACT.Sqrt, bias=pre[:, 0:1], scale=1.0
+            out=out_sb[:, ZCOL - 1 : ZCOL], in_=ssq[:, last : last + 1], func=ACT.Sqrt, bias=pre[:, 0:1], scale=1.0
         )
         nc.sync.dma_start(out=out_rows[:, 0 : 1 + 2 * BANK], in_=out_sb[:, ZCOL - 1 : ZCOL + 2 * BANK])

@@ -74,12 +74,15 @@ def tile_hypconvhyperboloid_w_kernel(tc, x, W_words, W_scales, b, out):
             )
 
         load_words(0, 0, N_OUT)
-        for half in range(2):
-            for quad in (0, 2, 1, 3):
-                nc.sync.dma_start(
-                    out=planes[32 * quad : 32 * quad + 16, half, :].bitcast(I32),
-                    in_=W_scales[4 * half : 4 * half + 4, 4 * quad : 4 * quad + 4, :].bitcast(I32),
-                )
+        for quad in (0, 2, 1, 3):
+            nc.sync.dma_start(
+                out=planes[32 * quad : 32 * quad + 16, 0, :].bitcast(I32),
+                in_=W_scales[0:4, 4 * quad : 4 * quad + 4, :].bitcast(I32),
+            )
+            nc.gpsimd.dma_start(
+                out=planes[32 * quad : 32 * quad + 16, 1, :].bitcast(F32),
+                in_=W_scales[4:8, 4 * quad : 4 * quad + 4, :].bitcast(F32),
+            )
         for g in range(1, WHOLE):
             load_words(g, 0, N_OUT)
         for lo, hi in CHUNKS:

@@ -23,6 +23,7 @@ XBASE = 456
 XCOLS = 342
 ZCOL = 8
 WHOLE = 6
+FIRST = 128
 CHUNKS = ((3072, 4096), (2048, 3072), (1024, 2048), (512, 1024), (0, 512))
 
 FLOPS = 2 * 128 * 4096 * 4096
@@ -183,6 +184,10 @@ def tile_hypconvhyperboloid_w_kernel(tc, x, W_words, W_scales, b, out):
             for j in banks:
                 z = out_sb[:, ZCOL + BANK * j : ZCOL + BANK * (j + 1)]
                 nc.vector.tensor_tensor(out=z, in0=acc[j][:], in1=z, op=ALU.add)
+            if i == last:
+                nc.sync.dma_start(
+                    out=out_rows[:, FIRST : 1 + 2 * BANK], in_=out_sb[:, ZCOL - 1 + FIRST : ZCOL + 2 * BANK]
+                )
             nc.scalar.activation(
                 out=junk[:, 0 : hi - lo],
                 in_=out_sb[:, ZCOL + lo : ZCOL + hi],
@@ -196,4 +201,4 @@ def tile_hypconvhyperboloid_w_kernel(tc, x, W_words, W_scales, b, out):
         nc.scalar.activation(
             out=out_sb[:, ZCOL - 1 : ZCOL], in_=ssq[:, last : last + 1], func=ACT.Sqrt, bias=pre[:, 0:1], scale=1.0
         )
-        nc.sync.dma_start(out=out_rows[:, 0 : 1 + 2 * BANK], in_=out_sb[:, ZCOL - 1 : ZCOL + 2 * BANK])
+        nc.scalar.dma_start(out=out_rows[:, 0:FIRST], in_=out_sb[:, ZCOL - 1 : ZCOL - 1 + FIRST])

@@ -46,8 +46,11 @@ def tile_hypconvhyperboloid_w_kernel(tc, x, W_words, W_scales, b, out):
         warm = keep.tile([P, 1], F32)
         ident = keep.tile([P, P], BF16)
         ipad = keep.tile([P, 2, 10, 10], BF16)
-        taps = keep.tile([P, 9, P], BF16)
+        pair = keep.tile([P, 2, 10, 8], BF16)
+        colsum = keep.tile([P, 2, 10, 8], BF16)
+        rowpair = keep.tile([P, 2, 8, 8], BF16)
         counts = keep.tile([P, P], F32)
+        bias_sb = keep.tile([P, N_OUT], BF16)
         xs = keep.tile([P, 4, XCOLS], BF16)
         tsq = keep.tile([P, 1], F32)
         grouped = keep.tile([P, GROUPS, P, 4], BF16, align_bytes=64)
@@ -62,8 +65,8 @@ def tile_hypconvhyperboloid_w_kernel(tc, x, W_words, W_scales, b, out):
         nc.vector.memset(planes[:, 0, :].bitcast(I32), 0)
         nc.vector.memset(planes[:, 1, :].bitcast(I32), 0)
         nc.scalar.dma_start(out=x_sb[:], in_=x_rows)
-        make_identity(nc, ident[:])
         nc.gpsimd.memset(b8[:].bitcast(F32), 0.0)
+        make_identity(nc, ident[:])
         nc.gpsimd.memset(consts[:, 0:1], -8.0)
         nc.gpsimd.memset(consts[:, 1:2], 1.0)
         nc.scalar.dma_start(out=b8[0:8, :], in_=b.rearrange("(j n) -> j n", j=8))
@@ -97,11 +100,16 @@ def tile_hypconvhyperboloid_w_kernel(tc, x, W_words, W_scales, b, out):
         nc.vector.tensor_copy(out=ipad[:, :, 1:9, 9:10], in_=ident4[:, :, :, 7:8])
         nc.vector.tensor_copy(out=ipad[:, :, 0:1, :], in_=ipad[:, :, 1:2, :])
         nc.vector.tensor_copy(out=ipad[:, :, 9:10, :], in_=ipad[:, :, 8:9, :])
-        for n in range(9):
-            nc.vector.tensor_copy(
-                out=taps[:, n, :].rearrange("p (b r q) -> p b r q", b=2, r=8),
-                in_=ipad[:, :, n // 3 : n // 3 + 8, n % 3 : n % 3 + 8],
-            )
+
+        nc.vector.tensor_tensor(out=pair[:], in0=ipad[:, :, :, 0:8], in1=ipad[:, :, :, 1:9], op=ALU.add)
+        nc.vector.tensor_tensor(out=colsum[:], in0=pair[:], in1=ipad[:, :, :, 2:10], op=ALU.add)
+        nc.vector.tensor_tensor(out=rowpair[:], in0=colsum[:, :, 0:8, :], in1=colsum[:, :, 1:9, :], op=ALU.add)
+        nc.vector.tensor_tensor(
+            out=counts[:].rearrange("p (b r q) -> p b r q", b=2, r=8),
+            in0=rowpair[:],
+            in1=colsum[:, :, 2:10, :],
+            op=ALU.add,
+        )
 
         nc.vector.tensor_copy(
             out=xs[:, :, XBASE // 4 : XBASE // 4 + C_IN // 4],
@@ -109,7 +117,19 @@ def tile_hypconvhyperboloid_w_kernel(tc, x, W_words, W_scales, b, out):
         )
         nc.vector.memset(xs[:, 0, XBASE // 4 : XBASE // 4 + 1], 0.0)
         nc.vector.tensor_tensor(out=tsq[:], in0=x_sb[:, 0:1], in1=x_sb[:, 0:1], op=ALU.mult)
-        nc.vector.tensor_reduce(out=counts[:], in_=taps[:].rearrange("p n x -> p x n"), axis=AX.X, op=ALU.add)
+
+        for half in range(4):
+            bp = psum.tile([P, 2 * BANK], BF16, tag="bank", name="bp%d" % half)
+            for e in range(2):
+                j = 2 * half + e
+                nc.tensor.matmul(
+                    out=bp[:, BANK * e : BANK * (e + 1)],
+                    lhsT=ident[:, j : j + 1].to_broadcast([P, P]),
+                    rhs=b8[:],
+                    start=True,
+                    stop=True,
+                )
+            nc.scalar.copy(out=bias_sb[:, 2 * BANK * half : 2 * BANK * (half + 1)], in_=bp[:])
 
         def gather_group(g):
             hp = psum.tile([P, 4, P], F32, tag="bank", name="hp%d" % g)
@@ -117,9 +137,9 @@ def tile_hypconvhyperboloid_w_kernel(tc, x, W_words, W_scales, b, out):
                 for n in (g, g + 1):
                     s = XBASE + 512 * g + t - SPACE * n
                     nc.tensor.matmul(
-                        out=hp[:, t, :],
+                        out=hp[:, t, :].rearrange("p (b r q) -> p b r q", b=2, r=8),
                         lhsT=xs[:, s % 4, s // 4 : s // 4 + P],
-                        rhs=taps[:, n, :],
+                        rhs=ipad[:, :, n // 3 : n // 3 + 8, n % 3 : n % 3 + 8],
                         start=(n == g),
                         stop=(n == g + 1),
                     )
@@ -138,27 +158,23 @@ def tile_hypconvhyperboloid_w_kernel(tc, x, W_words, W_scales, b, out):
         nc.scalar.activation(
             out=grouped[0:1, 0, :, 0], in_=tp[0:1, 0:P], func=ACT.Sqrt, bias=consts[0:1, 0:1], scale=1.0
         )
-        for g in range(2, GROUPS):
-            gather_group(g)
-        for half in range(2):
+        def quantize_half(half):
             nc.vector.quantize_mx(
                 out=hq[:, 512 * half : 512 * (half + 1)].bitcast(FP8X4),
                 scales=hs[:, 512 * half : 512 * (half + 1)],
                 in_=grouped[:, 4 * half : 4 * half + 4].rearrange("p g x t -> p (g x t)"),
             )
 
-        for j in range(8):
-            bp = psum.tile([P, BANK], F32, tag="bank", name="bp%d" % j)
-            nc.tensor.matmul(
-                out=bp[:], lhsT=ident[:, j : j + 1].to_broadcast([P, P]), rhs=b8[:], start=True, stop=True
-            )
-            dst = out_sb[:, ZCOL + BANK * j : ZCOL + BANK * (j + 1)]
-            if j % 2 == 0:
-                nc.vector.tensor_copy(out=dst, in_=bp[:])
-            else:
-                nc.scalar.copy(out=dst, in_=bp[:])
+        for g in range(2, 5):
+            gather_group(g)
+        quantize_half(0)
+        for g in range(5, GROUPS):
+            gather_group(g)
+        quantize_half(1)
 
-        acc = [psum.tile([P, BANK], F32, tag="bank", name="acc%d" % j) for j in range(8)]
+        acc = {}
+        for j in range(7, -1, -1):
+            acc[j] = psum.tile([P, BANK], F32, tag="bank", name="acc%d" % j)
 
         def mx_pass(g, j):
             nc.tensor.matmul_mx(
@@ -183,7 +199,9 @@ def tile_hypconvhyperboloid_w_kernel(tc, x, W_words, W_scales, b, out):
                     mx_pass(g, j)
             for j in banks:
                 z = out_sb[:, ZCOL + BANK * j : ZCOL + BANK * (j + 1)]
-                nc.vector.tensor_tensor(out=z, in0=acc[j][:], in1=z, op=ALU.add)
+                nc.vector.tensor_tensor(
+                    out=z, in0=acc[j][:], in1=bias_sb[:, BANK * j : BANK * (j + 1)], op=ALU.add
+                )
             if i == last:
                 nc.sync.dma_start(
                     out=out_rows[:, FIRST : 1 + 2 * BANK], in_=out_sb[:, ZCOL - 1 + FIRST : ZCOL + 2 * BANK]

@@ -24,7 +24,7 @@ XCOLS = 342
 ZCOL = 8
 WHOLE = 6
 FIRST = 128
-CHUNKS = ((3072, 4096), (2048, 3072), (1024, 2048), (512, 1024), (0, 512))
+CHUNKS = ((0, 1024), (1536, 2560), (3072, 4096), (1024, 1536), (2560, 3072))
 
 FLOPS = 2 * 128 * 4096 * 4096
 
@@ -202,18 +202,14 @@ def tile_hypconvhyperboloid_w_kernel(tc, x, W_words, W_scales, b, out):
                 nc.vector.tensor_tensor(
                     out=z, in0=acc[j][:], in1=bias_sb[:, BANK * j : BANK * (j + 1)], op=ALU.add
                 )
-            if i == last:
-                nc.sync.dma_start(
-                    out=out_rows[:, FIRST : 1 + 2 * BANK], in_=out_sb[:, ZCOL - 1 + FIRST : ZCOL + 2 * BANK]
-                )
+            first = max(1 + lo, FIRST)
+            nc.sync.dma_start(out=out_rows[:, first : 1 + hi], in_=out_sb[:, ZCOL - 1 + first : ZCOL + hi])
             nc.scalar.activation(
                 out=junk[:, 0 : hi - lo],
                 in_=out_sb[:, ZCOL + lo : ZCOL + hi],
                 func=ACT.Square,
                 accum_out=ssq[:, i : i + 1],
             )
-            if i < last - 1:
-                nc.sync.dma_start(out=out_rows[:, 1 + lo : 1 + hi], in_=out_sb[:, ZCOL + lo : ZCOL + hi])
         nc.vector.tensor_reduce(out=pre0[:], in_=ssq[:, 0:last], axis=AX.X, op=ALU.add)
         nc.vector.tensor_scalar_add(out=pre[:], in0=pre0[:], scalar1=1.0)
         nc.scalar.activation(

@@ -62,7 +62,6 @@ def tile_hypconvhyperboloid_w_kernel(tc, x, W_words, W_scales, b, out):
         pre0 = keep.tile([P, 1], F32)
         pre = keep.tile([P, 1], F32)
 
-        nc.vector.memset(planes[:, 0, :].bitcast(I32), 0)
         nc.vector.memset(planes[:, 1, :].bitcast(I32), 0)
         nc.scalar.dma_start(out=x_sb[:], in_=x_rows)
         nc.gpsimd.memset(b8[:].bitcast(F32), 0.0)
@@ -77,17 +76,18 @@ def tile_hypconvhyperboloid_w_kernel(tc, x, W_words, W_scales, b, out):
                 in_=W_words[g, :, lo:hi, :].rearrange("p n t -> p (n t)").bitcast(I32),
             )
 
-        load_words(0, 0, N_OUT)
-        for quad in (0, 2, 1, 3):
-            nc.sync.dma_start(
-                out=planes[32 * quad : 32 * quad + 16, 0, :].bitcast(I32),
-                in_=W_scales[0:4, 4 * quad : 4 * quad + 4, :].bitcast(I32),
-            )
-            nc.gpsimd.dma_start(
-                out=planes[32 * quad : 32 * quad + 16, 1, :].bitcast(F32),
-                in_=W_scales[4:8, 4 * quad : 4 * quad + 4, :].bitcast(F32),
-            )
-        for g in range(1, WHOLE):
+        for quads in ((2, 3), (0, 1)):
+            for quad in quads:
+                nc.sync.dma_start(
+                    out=planes[32 * quad : 32 * quad + 32, 0, :].bitcast(I32),
+                    in_=W_scales[:, 4 * quad : 4 * quad + 4, :].bitcast(I32),
+                )
+            for quad in quads:
+                nc.sync.dma_start(
+                    out=planes[32 * quad : 32 * quad + 16, 1, :].bitcast(I32),
+                    in_=W_scales[4:8, 4 * quad : 4 * quad + 4, :].bitcast(I32),
+                )
+        for g in range(WHOLE):
             load_words(g, 0, N_OUT)
         for lo, hi in CHUNKS:
             for g in range(WHOLE, GROUPS):

from contextlib import ExitStack

import concourse.mybir as mybir
from concourse.masks import make_identity

F32 = mybir.dt.float32
BF16 = mybir.dt.bfloat16
U8 = mybir.dt.uint8
U32 = mybir.dt.uint32
I32 = mybir.dt.int32
FP8X4 = mybir.dt.float8_e4m3fn_x4
ACT = mybir.ActivationFunctionType
ALU = mybir.AluOpType
AX = mybir.AxisListType

P = 128
C_IN = 456
SPACE = 455
GROUPS = 8
BANK = 512
N_OUT = 4096
XBASE = 456
XCOLS = 342
ZCOL = 8
WHOLE = 6
FIRST = 128
CHUNKS = ((0, 1024), (1536, 2560), (3072, 4096), (1024, 1536), (2560, 3072))

FLOPS = 2 * 128 * 4096 * 4096


def tile_hypconvhyperboloid_w_kernel(tc, x, W_words, W_scales, b, out):
    nc = tc.nc
    x_rows = x.flatten_outer_dims()
    out_rows = out.flatten_outer_dims()
    with ExitStack() as ctx:
        keep = ctx.enter_context(tc.tile_pool(name="keep", bufs=1))
        psum = ctx.enter_context(tc.psum_pool(name="psum", bufs=8))
        ctx.enter_context(tc.manual_schedule())

        planes = keep.tile([P, 2, N_OUT], U8, align_bytes=64)
        w = [keep.tile([P, N_OUT], U32, name="w%d" % g, align_bytes=64) for g in range(GROUPS)]
        x_sb = keep.tile([P, C_IN], BF16)
        b8 = keep.tile([P, BANK], BF16)
        consts = keep.tile([P, 2], F32)
        warm = keep.tile([P, 1], F32)
        ident = keep.tile([P, P], BF16)
        ipad = keep.tile([P, 2, 10, 10], BF16)
        pair = keep.tile([P, 2, 10, 8], BF16)
        colsum = keep.tile([P, 2, 10, 8], BF16)
        rowpair = keep.tile([P, 2, 8, 8], BF16)
        counts = keep.tile([P, P], F32)
        bias_sb = keep.tile([P, N_OUT], BF16)
        xs = keep.tile([P, 4, XCOLS], BF16)
        tsq = keep.tile([P, 1], F32)
        grouped = keep.tile([P, GROUPS, P, 4], BF16, align_bytes=64)
        hq = keep.tile([P, GROUPS * P], U32, align_bytes=64)
        hs = keep.tile([P, GROUPS * P], U8, align_bytes=64)
        out_sb = keep.tile([P, ZCOL + N_OUT], F32)
        junk = keep.tile([P, 2 * BANK], F32)
        ssq = keep.tile([P, GROUPS], F32)
        pre0 = keep.tile([P, 1], F32)
        pre = keep.tile([P, 1], F32)

        nc.vector.memset(planes[:, 1, :].bitcast(I32), 0)
        nc.scalar.dma_start(out=x_sb[:], in_=x_rows)
        nc.gpsimd.memset(b8[:].bitcast(F32), 0.0)
        make_identity(nc, ident[:])
        nc.gpsimd.memset(consts[:, 0:1], -8.0)
        nc.gpsimd.memset(consts[:, 1:2], 1.0)
        nc.scalar.dma_start(out=b8[0:8, :], in_=b.rearrange("(j n) -> j n", j=8))
        nc.scalar.activation(out=warm[:], in_=consts[:, 1:2], func=ACT.Sqrt)
        def load_words(g, lo, hi):
            nc.sync.dma_start(
                out=w[g][:, lo:hi].bitcast(I32),
                in_=W_words[g, :, lo:hi, :].rearrange("p n t -> p (n t)").bitcast(I32),
            )

        for quads in ((2, 3), (0, 1)):
            for quad in quads:
                nc.sync.dma_start(
                    out=planes[32 * quad : 32 * quad + 32, 0, :].bitcast(I32),
                    in_=W_scales[:, 4 * quad : 4 * quad + 4, :].bitcast(I32),
                )
            for quad in quads:
                nc.sync.dma_start(
                    out=planes[32 * quad : 32 * quad + 16, 1, :].bitcast(I32),
                    in_=W_scales[4:8, 4 * quad : 4 * quad + 4, :].bitcast(I32),
                )
        for g in range(WHOLE):
            load_words(g, 0, N_OUT)
        for lo, hi in CHUNKS:
            for g in range(WHOLE, GROUPS):
                load_words(g, lo, hi)

        nc.vector.memset(xs[:].rearrange("p f c -> p (f c)").bitcast(I32), 0)
        ident4 = ident[:].rearrange("p (b r q) -> p b r q", b=2, r=8)
        nc.vector.tensor_copy(out=ipad[:, :, 1:9, 1:9], in_=ident4)
        nc.vector.tensor_copy(out=ipad[:, :, 1:9, 0:1], in_=ident4[:, :, :, 0:1])
        nc.vector.tensor_copy(out=ipad[:, :, 1:9, 9:10], in_=ident4[:, :, :, 7:8])
        nc.vector.tensor_copy(out=ipad[:, :, 0:1, :], in_=ipad[:, :, 1:2, :])
        nc.vector.tensor_copy(out=ipad[:, :, 9:10, :], in_=ipad[:, :, 8:9, :])

        nc.vector.tensor_tensor(out=pair[:], in0=ipad[:, :, :, 0:8], in1=ipad[:, :, :, 1:9], op=ALU.add)
        nc.vector.tensor_tensor(out=colsum[:], in0=pair[:], in1=ipad[:, :, :, 2:10], op=ALU.add)
        nc.vector.tensor_tensor(out=rowpair[:], in0=colsum[:, :, 0:8, :], in1=colsum[:, :, 1:9, :], op=ALU.add)
        nc.vector.tensor_tensor(
            out=counts[:].rearrange("p (b r q) -> p b r q", b=2, r=8),
            in0=rowpair[:],
            in1=colsum[:, :, 2:10, :],
            op=ALU.add,
        )

        nc.vector.tensor_copy(
            out=xs[:, :, XBASE // 4 : XBASE // 4 + C_IN // 4],
            in_=x_sb[:].rearrange("p (c f) -> p f c", f=4),
        )
        nc.vector.memset(xs[:, 0, XBASE // 4 : XBASE // 4 + 1], 0.0)
        nc.vector.tensor_tensor(out=tsq[:], in0=x_sb[:, 0:1], in1=x_sb[:, 0:1], op=ALU.mult)

        for half in range(4):
            bp = psum.tile([P, 2 * BANK], BF16, tag="bank", name="bp%d" % half)
            for e in range(2):
                j = 2 * half + e
                nc.tensor.matmul(
                    out=bp[:, BANK * e : BANK * (e + 1)],
                    lhsT=ident[:, j : j + 1].to_broadcast([P, P]),
                    rhs=b8[:],
                    start=True,
                    stop=True,
                )
            nc.scalar.copy(out=bias_sb[:, 2 * BANK * half : 2 * BANK * (half + 1)], in_=bp[:])

        def gather_group(g):
            hp = psum.tile([P, 4, P], F32, tag="bank", name="hp%d" % g)
            for t in range(4):
                for n in (g, g + 1):
                    s = XBASE + 512 * g + t - SPACE * n
                    nc.tensor.matmul(
                        out=hp[:, t, :].rearrange("p (b r q) -> p b r q", b=2, r=8),
                        lhsT=xs[:, s % 4, s // 4 : s // 4 + P],
                        rhs=ipad[:, :, n // 3 : n // 3 + 8, n % 3 : n % 3 + 8],
                        start=(n == g),
                        stop=(n == g + 1),
                    )
            src = hp[:].rearrange("p t x -> p x t")
            if g % 2 == 0:
                nc.vector.tensor_copy(out=grouped[:, g], in_=src)
            else:
                nc.scalar.copy(out=grouped[:, g], in_=src)

        gather_group(0)
        gather_group(1)
        tp = psum.tile([P, BANK], F32, tag="bank")
        nc.tensor.matmul(
            out=tp[:, 0:P], lhsT=tsq[:, 0:1].to_broadcast([P, P]), rhs=counts[:], start=True, stop=True
        )
        nc.scalar.activation(
            out=grouped[0:1, 0, :, 0], in_=tp[0:1, 0:P], func=ACT.Sqrt, bias=consts[0:1, 0:1], scale=1.0
        )
        def quantize_half(half):
            nc.vector.quantize_mx(
                out=hq[:, 512 * half : 512 * (half + 1)].bitcast(FP8X4),
                scales=hs[:, 512 * half : 512 * (half + 1)],
                in_=grouped[:, 4 * half : 4 * half + 4].rearrange("p g x t -> p (g x t)"),
            )

        for g in range(2, 5):
            gather_group(g)
        quantize_half(0)
        for g in range(5, GROUPS):
            gather_group(g)
        quantize_half(1)

        acc = {}
        for j in range(7, -1, -1):
            acc[j] = psum.tile([P, BANK], F32, tag="bank", name="acc%d" % j)

        def mx_pass(g, j):
            nc.tensor.matmul_mx(
                out=acc[j][:],
                lhsT=hq[:, P * g : P * (g + 1)].bitcast(FP8X4),
                lhsT_scale=hs[:, P * g : P * (g + 1)],
                rhs=w[g][:, BANK * j : BANK * (j + 1)].bitcast(FP8X4),
                rhs_scale=planes[4 * (g % 4) : P, g // 4, BANK * j : BANK * (j + 1)],
                start=(g == 0),
                stop=(g == GROUPS - 1),
            )

        for g in range(WHOLE):
            for j in range(7, -1, -1):
                mx_pass(g, j)

        last = len(CHUNKS) - 1
        for i, (lo, hi) in enumerate(CHUNKS):
            banks = range(hi // BANK - 1, lo // BANK - 1, -1)
            for g in range(WHOLE, GROUPS):
                for j in banks:
                    mx_pass(g, j)
            for j in banks:
                z = out_sb[:, ZCOL + BANK * j : ZCOL + BANK * (j + 1)]
                nc.vector.tensor_tensor(
                    out=z, in0=acc[j][:], in1=bias_sb[:, BANK * j : BANK * (j + 1)], op=ALU.add
                )
            first = max(1 + lo, FIRST)
            nc.sync.dma_start(out=out_rows[:, first : 1 + hi], in_=out_sb[:, ZCOL - 1 + first : ZCOL + hi])
            nc.scalar.activation(
                out=junk[:, 0 : hi - lo],
                in_=out_sb[:, ZCOL + lo : ZCOL + hi],
                func=ACT.Square,
                accum_out=ssq[:, i : i + 1],
            )
        nc.vector.tensor_reduce(out=pre0[:], in_=ssq[:, 0:last], axis=AX.X, op=ALU.add)
        nc.vector.tensor_scalar_add(out=pre[:], in0=pre0[:], scalar1=1.0)
        nc.scalar.activation(
            out=out_sb[:, ZCOL - 1 : ZCOL], in_=ssq[:, last : last + 1], func=ACT.Sqrt, bias=pre[:, 0:1], scale=1.0
        )
        nc.scalar.dma_start(out=out_rows[:, 0:FIRST], in_=out_sb[:, ZCOL - 1 : ZCOL - 1 + FIRST])
